import numpy as np
import ml_dtypes


def mxq(x, axis, fmt="e4m3"):
    dtype, down = {"e4m3": (ml_dtypes.float8_e4m3fn, 7), "e5m2": (ml_dtypes.float8_e5m2, 14)}[fmt]
    v = np.moveaxis(np.asarray(x, np.float32).astype(ml_dtypes.bfloat16).astype(np.float64), axis, -1)
    blocks = v.reshape(v.shape[:-1] + (-1, 32))
    amax = np.abs(blocks).max(-1, keepdims=True)
    byte = np.maximum(np.where(amax > 0, np.frexp(amax)[1] - 1 + 127, 0) - down, 1)
    scale = np.exp2(byte - 127.0)
    codes = (blocks / scale).astype(np.float32).astype(dtype).astype(np.float64)
    return np.moveaxis((codes * scale).reshape(v.shape), -1, axis)


WIDE = False


def mx_kscale(k):
    if not WIDE:
        return np.ones(k)
    levels = np.array([10, -10, 5, -5, 0])
    a = np.random.permutation(np.resize(levels, k // 512 * 4)).reshape(k // 512, 4)
    idx = np.arange(k)
    return np.exp2(a[idx // 512, idx % 128 // 32])


BF16 = ml_dtypes.bfloat16


def bf(x):
    return np.asarray(x, np.float32).astype(BF16)


def f64(x):
    return np.asarray(x).astype(np.float64)


E2M1 = np.array([0.0, 0.5, 1.0, 1.5, 2.0, 3.0, 4.0, 6.0, -0.0, -0.5, -1.0, -1.5, -2.0, -3.0, -4.0, -6.0])


def pack_weight(w, fmt):
    k, n = w.shape
    w = f64(bf(w)).reshape(k // 32, 32, n)
    amax = np.abs(w).max(1)
    if fmt == "e4m3":
        byte = np.frexp(amax)[1] - 1 + 127 - 7
    else:
        mant, ex = np.frexp(amax / 6.0)
        byte = np.where(mant > 0.5, ex, ex - 1) + 127
    byte = np.clip(np.where(amax > 0, byte, 1), 1, 254)
    scaled = (w * np.exp2(127.0 - byte)[:, None, :]).reshape(k, n).astype(np.float32)
    by_word = np.ascontiguousarray(scaled.reshape(k // 512, 128, 4, n).transpose(0, 1, 3, 2))
    if fmt == "e4m3":
        words = by_word.astype(ml_dtypes.float8_e4m3fn).view(np.uint8)
    else:
        c = by_word.astype(ml_dtypes.float4_e2m1fn).view(np.uint8) & 0xF
        words = c[..., 0::2] | (c[..., 1::2] << 4)
    return np.ascontiguousarray(words), np.ascontiguousarray(byte.astype(np.uint8).reshape(k // 512, 16, n))


def unpack_weight(words, scales, fmt):
    g, p, n, _ = words.shape
    if fmt == "e4m3":
        vals = np.ascontiguousarray(words).view(ml_dtypes.float8_e4m3fn).astype(np.float64)
    else:
        nib = np.empty((g, p, n, 4), np.uint8)
        nib[..., 0::2] = words & 0xF
        nib[..., 1::2] = words >> 4
        vals = E2M1[nib]
    vals = vals * np.repeat(np.exp2(scales.astype(np.float64) - 127.0), 8, axis=1)[..., None]
    return vals.transpose(0, 1, 3, 2).reshape(g * 512, n)


B, IN, OUT = 128, 1536, 1536
G = OUT // 3
FMT = "e4m3"


def _hamilton_block(r, i, j, k):
    col_r = np.concatenate([r, i, j, k], axis=0)
    col_i = np.concatenate([i, r, -k, j], axis=0)
    col_j = np.concatenate([j, k, r, -i], axis=0)
    col_k = np.concatenate([k, -j, i, r], axis=0)
    return np.concatenate([col_r, col_i, col_j, col_k], axis=1)


def setup_inputs():
    s = mx_kscale(4 * IN)[:IN]
    c = 1.0 / np.sqrt(4 * IN)
    x = bf(np.random.standard_normal((B, 4 * IN)) * np.tile(s, 4))
    r_words, r_scales = pack_weight(np.random.standard_normal((IN, OUT)) * c / s[:, None], FMT)
    i_words, i_scales = pack_weight(np.random.standard_normal((IN, OUT)) * c / s[:, None], FMT)
    j_words, j_scales = pack_weight(np.random.standard_normal((IN, OUT)) * c / s[:, None], FMT)
    k_words, k_scales = pack_weight(np.random.standard_normal((IN, OUT)) * c / s[:, None], FMT)
    return {"x": x,
            "r_weight_words": r_words, "r_weight_scales": r_scales,
            "i_weight_words": i_words, "i_weight_scales": i_scales,
            "j_weight_words": j_words, "j_weight_scales": j_scales,
            "k_weight_words": k_words, "k_weight_scales": k_scales,
            "drop": 0}


def reference(x, r_weight_words, r_weight_scales, i_weight_words, i_weight_scales,
              j_weight_words, j_weight_scales, k_weight_words, k_weight_scales, drop):
    xq = mxq(f64(x), 1, "e4m3")
    r = unpack_weight(r_weight_words, r_weight_scales, FMT)
    i = unpack_weight(i_weight_words, i_weight_scales, FMT)
    j = unpack_weight(j_weight_words, j_weight_scales, FMT)
    k = unpack_weight(k_weight_words, k_weight_scales, FMT)
    outputs = []
    for c in range(3):
        sl = slice(c * G, (c + 1) * G)
        W = _hamilton_block(r[:, sl], i[:, sl], j[:, sl], k[:, sl])
        outputs.append(xq @ W)
    return tuple(outputs)

@@ -1,0 +1,222 @@
+from contextlib import ExitStack
+
+import concourse.mybir as mybir
+from concourse.masks import make_identity
+
+F32 = mybir.dt.float32
+BF16 = mybir.dt.bfloat16
+I32 = mybir.dt.int32
+U32 = mybir.dt.uint32
+U8 = mybir.dt.uint8
+FP8X4 = mybir.dt.float8_e4m3fn_x4
+
+P = 128
+QUARTERS = 4
+GROUPS = 3
+GATES = 3
+N_TILE = 512
+NEGATED = ((1, 3), (2, 1), (3, 2))
+
+FLOPS = 2 * 128 * 6144 * 6144
+
+
+def tile_quaternionlinearautograd_w_kernel(
+    tc, x,
+    r_weight_words, r_weight_scales, i_weight_words, i_weight_scales,
+    j_weight_words, j_weight_scales, k_weight_words, k_weight_scales,
+    drop, out_0, out_1, out_2,
+):
+    nc = tc.nc
+    words = (r_weight_words, i_weight_words, j_weight_words, k_weight_words)
+    scales = (r_weight_scales, i_weight_scales, j_weight_scales, k_weight_scales)
+    outs = (out_0, out_1, out_2)
+
+    with ExitStack() as ctx:
+        keep = ctx.enter_context(tc.tile_pool(name="keep", bufs=1))
+        psum = ctx.enter_context(tc.psum_pool(name="psum", bufs=1))
+        ctx.enter_context(tc.manual_schedule())
+
+        ident = keep.tile([P, P], F32, name="ident")
+        planes = [keep.tile([P, GATES * N_TILE], U8, name="planes%d" % w, align_bytes=64) for w in range(4)]
+        x_sb = {}
+        for g in range(GROUPS):
+            for h in range(2):
+                x_sb[(g, h)] = keep.tile([P, 2, 512], BF16, name="x_sb%d_%d" % (g, h))
+        w_sb = {}
+        for c in range(GATES):
+            for g in range(GROUPS):
+                for w in range(4):
+                    w_sb[(w, g, c)] = keep.tile([P, 4 * N_TILE], U8, name="w_sb%d_%d_%d" % (w, g, c), align_bytes=64)
+        grouped = [keep.tile([P, 4, P, 4], BF16, name="grouped%d" % g, align_bytes=64) for g in range(GROUPS)]
+        minus = [keep.tile([P, 3, P, 4], BF16, name="minus%d" % g, align_bytes=64) for g in range(GROUPS)]
+        x_codes = [keep.tile([P, 7, P], U32, name="x_codes%d" % g, align_bytes=64) for g in range(GROUPS)]
+        x_scales = [keep.tile([P, 7, P], U8, name="x_scales%d" % g, align_bytes=64) for g in range(GROUPS)]
+        out_sb = [keep.tile([P, 4 * N_TILE], F32, name="out_sb%d" % c) for c in range(GATES)]
+
+        for w in range(4):
+            nc.vector.memset(planes[w][:].bitcast(I32), 0)
+        make_identity(nc, ident[:])
+
+        x_view = x.rearrange("b (a g k) -> g a b k", a=QUARTERS, g=GROUPS)
+
+        def load_x(g, h):
+            nc.sync.dma_start(
+                out=x_sb[(g, h)][:],
+                in_=x_view[g, 2 * h:2 * h + 2].rearrange("a b k -> b a k"),
+            )
+
+        def load_scales(w):
+            src = scales[w].bitcast(I32)
+            for q in range(4):
+                nc.sync.dma_start(
+                    out=planes[w][32 * q:32 * q + 4 * GROUPS, :].bitcast(I32),
+                    in_=src[:, 4 * q:4 * q + 4, :],
+                )
+
+        def load_words(w, g, c):
+            src = words[w][g].rearrange("p n t -> p (n t)")
+            nc.sync.dma_start(
+                out=w_sb[(w, g, c)][:].bitcast(I32),
+                in_=src[:, 4 * N_TILE * c:4 * N_TILE * (c + 1)].bitcast(I32),
+            )
+
+        load_x(0, 0)
+        load_x(0, 1)
+        load_scales(0)
+        load_words(0, 0, 0)
+        load_scales(1)
+        load_words(1, 0, 0)
+        load_x(1, 0)
+        load_x(1, 1)
+        load_x(2, 0)
+        load_x(2, 1)
+        load_scales(2)
+        load_words(2, 0, 0)
+        load_scales(3)
+        load_words(3, 0, 0)
+        for c in range(GATES):
+            for g in range(GROUPS):
+                for w in range(4):
+                    if c > 0 or g > 0:
+                        load_words(w, g, c)
+
+        def transposes(g, h, bank):
+            xt = psum.tile([P, 4, P], F32, name="xt%d_%d" % (g, h), tag="bank%d" % bank)
+            xw = x_sb[(g, h)][:].bitcast(F32)
+            for al in range(2):
+                for u in range(2):
+                    nc.tensor.transpose(xt[:, 2 * al + u, :], xw[:, al, u:256:2], ident[:])
+            return xt
+
+        def regroup(g, h, xt):
+            dst = grouped[g][:].bitcast(F32)[:, 2 * h:2 * h + 2]
+            src = xt[:].rearrange("p (a u) r -> p a r u", u=2)
+            if h == 0:
+                nc.vector.tensor_copy(out=dst, in_=src)
+            else:
+                nc.scalar.copy(out=dst, in_=src)
+
+        def quantise(g, src, first, count):
+            nc.vector.quantize_mx(
+                out=x_codes[g][:, first:first + count, :].rearrange("p s r -> p (s r)").bitcast(FP8X4),
+                scales=x_scales[g][:, first:first + count, :].rearrange("p s r -> p (s r)"),
+                in_=src.rearrange("p a r t -> p (a r t)"),
+            )
+
+        def negate(g):
+            nc.vector.tensor_scalar(
+                out=minus[g][:].rearrange("p a r t -> p (a r t)"),
+                in0=grouped[g][:, 1:4].rearrange("p a r t -> p (a r t)"),
+                scalar1=-1.0, scalar2=None, op0=mybir.AluOpType.mult,
+            )
+
+        def quantise_minus(g):
+            quantise(g, minus[g][:, 0:2], 4, 2)
+            quantise(g, minus[g][:, 2:3], 6, 1)
+
+        done = {}
+        acc = {}
+
+        def mx_pass(w, g, c, a):
+            b = a ^ w
+            n = done.get((c, b), 0)
+            done[(c, b)] = n + 1
+            slot = a + 3 if (w, a) in NEGATED else a
+            nc.tensor.matmul_mx(
+                out=acc[(c, b)][:],
+                lhsT=x_codes[g][:, slot, :].bitcast(FP8X4),
+                lhsT_scale=x_scales[g][:, slot, :],
+                rhs=w_sb[(w, g, c)][:].bitcast(FP8X4),
+                rhs_scale=planes[w][4 * g:P, N_TILE * c:N_TILE * (c + 1)],
+                start=(n == 0),
+                stop=(n == QUARTERS * GROUPS - 1),
+            )
+
+        def chunk(w, g, c):
+            order = [a for a in range(QUARTERS) if (w, a) not in NEGATED] + [a for a in range(QUARTERS) if (w, a) in NEGATED]
+            for a in order:
+                mx_pass(w, g, c, a)
+
+        def leave(c, b):
+            dst = out_sb[c][:, N_TILE * b:N_TILE * (b + 1)]
+            if b % 2 == 0:
+                nc.vector.tensor_copy(out=dst, in_=acc[(c, b)][:])
+            else:
+                nc.scalar.copy(out=dst, in_=acc[(c, b)][:])
+
+        def open_gate(c):
+            for b in range(4):
+                acc[(c, b)] = psum.tile([P, N_TILE], F32, name="acc%d_%d" % (c, b), tag="bank%d" % (4 * (c % 2) + b))
+
+        open_gate(0)
+        xt00 = transposes(0, 0, 4)
+        xt01 = transposes(0, 1, 5)
+        regroup(0, 0, xt00)
+        regroup(0, 1, xt01)
+        quantise(0, grouped[0][:, 0:2], 0, 2)
+        quantise(0, grouped[0][:, 2:4], 2, 2)
+        negate(0)
+        quantise_minus(0)
+        chunk(0, 0, 0)
+        chunk(1, 0, 0)
+        xt10 = transposes(1, 0, 6)
+        xt11 = transposes(1, 1, 7)
+        xt20 = transposes(2, 0, 4)
+        xt21 = transposes(2, 1, 5)
+        regroup(1, 0, xt10)
+        regroup(1, 1, xt11)
+        regroup(2, 0, xt20)
+        regroup(2, 1, xt21)
+        quantise(1, grouped[1][:], 0, 4)
+        negate(1)
+        quantise(2, grouped[2][:], 0, 4)
+        quantise_minus(1)
+        negate(2)
+        quantise_minus(2)
+        chunk(2, 0, 0)
+        chunk(3, 0, 0)
+        for g in range(1, GROUPS):
+            for w in range(4):
+                chunk(w, g, 0)
+        for b in range(4):
+            leave(0, b)
+        nc.sync.dma_start(out=outs[0][:, :], in_=out_sb[0][:])
+
+        open_gate(1)
+        for g in range(GROUPS):
+            for w in range(4):
+                chunk(w, g, 1)
+        for b in range(4):
+            leave(1, b)
+        nc.sync.dma_start(out=outs[1][:, :], in_=out_sb[1][:])
+
+        open_gate(2)
+        for b in range(4):
+            for g in range(GROUPS):
+                for w in range(4):
+                    mx_pass(w, g, 2, b ^ w)
+            leave(2, b)
+            nc.sync.dma_start(
+                out=outs[2][:, N_TILE * b:N_TILE * (b + 1)],
+                in_=out_sb[2][:, N_TILE * b:N_TILE * (b + 1)],
+            )

@@ -66,12 +66,12 @@ def tile_quaternionlinearautograd_w_kernel(
             )
 
         def load_scales(w):
-            src = scales[w].bitcast(I32)
             for q in range(4):
-                nc.sync.dma_start(
-                    out=planes[w][32 * q:32 * q + 4 * GROUPS, :].bitcast(I32),
-                    in_=src[:, 4 * q:4 * q + 4, :],
-                )
+                dst = planes[w][32 * q:32 * q + 4 * GROUPS, :]
+                if w == 0:
+                    nc.sync.dma_start(out=dst.bitcast(I32), in_=scales[w].bitcast(I32)[:, 4 * q:4 * q + 4, :])
+                else:
+                    nc.gpsimd.dma_start(out=dst.bitcast(F32), in_=scales[w].bitcast(F32)[:, 4 * q:4 * q + 4, :])
 
         def load_words(w, g, c):
             src = words[w][g].rearrange("p n t -> p (n t)")
@@ -84,20 +84,16 @@ def tile_quaternionlinearautograd_w_kernel(
         load_x(0, 1)
         load_scales(0)
         load_words(0, 0, 0)
-        load_scales(1)
-        load_words(1, 0, 0)
         load_x(1, 0)
         load_x(1, 1)
         load_x(2, 0)
         load_x(2, 1)
-        load_scales(2)
-        load_words(2, 0, 0)
-        load_scales(3)
-        load_words(3, 0, 0)
+        for w in range(1, 4):
+            load_scales(w)
         for c in range(GATES):
-            for g in range(GROUPS):
-                for w in range(4):
-                    if c > 0 or g > 0:
+            for w in range(4):
+                for g in range(GROUPS):
+                    if (w, g, c) != (0, 0, 0):
                         load_words(w, g, c)
 
         def transposes(g, h, bank):
@@ -178,33 +174,33 @@ def tile_quaternionlinearautograd_w_kernel(
         negate(0)
         quantise_minus(0)
         chunk(0, 0, 0)
-        chunk(1, 0, 0)
         xt10 = transposes(1, 0, 6)
         xt11 = transposes(1, 1, 7)
         xt20 = transposes(2, 0, 4)
         xt21 = transposes(2, 1, 5)
         regroup(1, 0, xt10)
         regroup(1, 1, xt11)
+        quantise(1, grouped[1][:, 0:2], 0, 2)
+        quantise(1, grouped[1][:, 2:4], 2, 2)
         regroup(2, 0, xt20)
         regroup(2, 1, xt21)
-        quantise(1, grouped[1][:], 0, 4)
+        quantise(2, grouped[2][:, 0:2], 0, 2)
+        quantise(2, grouped[2][:, 2:4], 2, 2)
         negate(1)
-        quantise(2, grouped[2][:], 0, 4)
         quantise_minus(1)
         negate(2)
         quantise_minus(2)
-        chunk(2, 0, 0)
-        chunk(3, 0, 0)
-        for g in range(1, GROUPS):
-            for w in range(4):
-                chunk(w, g, 0)
+        for w in range(4):
+            for g in range(GROUPS):
+                if (w, g) != (0, 0):
+                    chunk(w, g, 0)
         for b in range(4):
             leave(0, b)
         nc.sync.dma_start(out=outs[0][:, :], in_=out_sb[0][:])
 
         open_gate(1)
-        for g in range(GROUPS):
-            for w in range(4):
+        for w in range(4):
+            for g in range(GROUPS):
                 chunk(w, g, 1)
         for b in range(4):
             leave(1, b)

@@ -13,8 +13,8 @@ FP8X4 = mybir.dt.float8_e4m3fn_x4
 P = 128
 QUARTERS = 4
 GROUPS = 3
-GATES = 3
 N_TILE = 512
+PASSES = QUARTERS * GROUPS
 NEGATED = ((1, 3), (2, 1), (3, 2))
 
 FLOPS = 2 * 128 * 6144 * 6144
@@ -37,29 +37,16 @@ def tile_quaternionlinearautograd_w_kernel(
         ctx.enter_context(tc.manual_schedule())
 
         ident = keep.tile([P, P], F32, name="ident")
-        planes = [keep.tile([P, GATES * N_TILE], U8, name="planes%d" % w, align_bytes=64) for w in range(4)]
-        x_sb = {}
-        for g in range(GROUPS):
-            for h in range(2):
-                x_sb[(g, h)] = keep.tile([P, 2, 512], BF16, name="x_sb%d_%d" % (g, h))
-        w_sb = {}
-        for c in range(GATES):
-            for g in range(GROUPS):
-                for w in range(4):
-                    w_sb[(w, g, c)] = keep.tile([P, 4 * N_TILE], U8, name="w_sb%d_%d_%d" % (w, g, c), align_bytes=64)
-        grouped = [keep.tile([P, 4, P, 4], BF16, name="grouped%d" % g, align_bytes=64) for g in range(GROUPS)]
-        minus = [keep.tile([P, 3, P, 4], BF16, name="minus%d" % g, align_bytes=64) for g in range(GROUPS)]
-        x_codes = [keep.tile([P, 7, P], U32, name="x_codes%d" % g, align_bytes=64) for g in range(GROUPS)]
-        x_scales = [keep.tile([P, 7, P], U8, name="x_scales%d" % g, align_bytes=64) for g in range(GROUPS)]
-        out_sb = [keep.tile([P, 4 * N_TILE], F32, name="out_sb%d" % c) for c in range(GATES)]
-
+        planes = [keep.tile([P, 3 * N_TILE], U8, name="planes%d" % w, align_bytes=64) for w in range(4)]
         for w in range(4):
             nc.vector.memset(planes[w][:].bitcast(I32), 0)
         make_identity(nc, ident[:])
 
         x_view = x.rearrange("b (a g k) -> g a b k", a=QUARTERS, g=GROUPS)
+        x_sb = {}
 
         def load_x(g, h):
+            x_sb[(g, h)] = keep.tile([P, 2, 512], BF16, name="x_sb%d_%d" % (g, h))
             nc.sync.dma_start(
                 out=x_sb[(g, h)][:],
                 in_=x_view[g, 2 * h:2 * h + 2].rearrange("a b k -> b a k"),
@@ -73,146 +60,162 @@ def tile_quaternionlinearautograd_w_kernel(
                 else:
                     nc.gpsimd.dma_start(out=dst.bitcast(F32), in_=scales[w].bitcast(F32)[:, 4 * q:4 * q + 4, :])
 
-        def load_words(w, g, c):
+        w_sb = {}
+
+        def load_words(w, g, c_first, c_count):
+            t = keep.tile([P, 4 * N_TILE * c_count], U8, name="w_sb%d_%d_%d" % (w, g, c_first), align_bytes=64)
             src = words[w][g].rearrange("p n t -> p (n t)")
             nc.sync.dma_start(
-                out=w_sb[(w, g, c)][:].bitcast(I32),
-                in_=src[:, 4 * N_TILE * c:4 * N_TILE * (c + 1)].bitcast(I32),
+                out=t[:].bitcast(I32),
+                in_=src[:, 4 * N_TILE * c_first:4 * N_TILE * (c_first + c_count)].bitcast(I32),
             )
+            for c in range(c_count):
+                w_sb[(w, g, c_first + c)] = (t, 4 * N_TILE * c)
 
         load_x(0, 0)
         load_x(0, 1)
         load_scales(0)
-        load_words(0, 0, 0)
+        load_words(0, 0, 0, 1)
         load_x(1, 0)
         load_x(1, 1)
         load_x(2, 0)
         load_x(2, 1)
         for w in range(1, 4):
             load_scales(w)
-        for c in range(GATES):
-            for w in range(4):
-                for g in range(GROUPS):
-                    if (w, g, c) != (0, 0, 0):
-                        load_words(w, g, c)
+        load_words(0, 1, 0, 2)
+        load_words(0, 2, 0, 2)
+        load_words(0, 0, 1, 1)
+        for w in range(1, 4):
+            for g in range(GROUPS):
+                load_words(w, g, 0, 2)
+        for w in range(4):
+            for g in range(GROUPS):
+                load_words(w, g, 2, 1)
+
+        xt = {}
+        grouped = {}
+        operand = {}
 
         def transposes(g, h, bank):
-            xt = psum.tile([P, 4, P], F32, name="xt%d_%d" % (g, h), tag="bank%d" % bank)
+            xt[(g, h)] = psum.tile([P, 4, P], F32, name="xt%d_%d" % (g, h), tag="bank%d" % bank)
             xw = x_sb[(g, h)][:].bitcast(F32)
             for al in range(2):
                 for u in range(2):
-                    nc.tensor.transpose(xt[:, 2 * al + u, :], xw[:, al, u:256:2], ident[:])
-            return xt
+                    nc.tensor.transpose(xt[(g, h)][:, 2 * al + u, :], xw[:, al, u:256:2], ident[:])
 
-        def regroup(g, h, xt):
-            dst = grouped[g][:].bitcast(F32)[:, 2 * h:2 * h + 2]
-            src = xt[:].rearrange("p (a u) r -> p a r u", u=2)
+        def regroup(g, h):
+            grouped[(g, h)] = keep.tile([P, 2, P, 4], BF16, name="grouped%d_%d" % (g, h), align_bytes=64)
+            dst = grouped[(g, h)][:].bitcast(F32)
+            src = xt[(g, h)][:].rearrange("p (a u) r -> p a r u", u=2)
             if h == 0:
                 nc.vector.tensor_copy(out=dst, in_=src)
             else:
                 nc.scalar.copy(out=dst, in_=src)
 
-        def quantise(g, src, first, count):
+        def quantise(g, src, quarters, negated):
+            n = len(quarters)
+            label = "%d_%d_%d" % (g, quarters[0], negated)
+            codes = keep.tile([P, n, P], U32, name="codes" + label, align_bytes=64)
+            plane = keep.tile([P, n, P], U8, name="plane" + label, align_bytes=64)
             nc.vector.quantize_mx(
-                out=x_codes[g][:, first:first + count, :].rearrange("p s r -> p (s r)").bitcast(FP8X4),
-                scales=x_scales[g][:, first:first + count, :].rearrange("p s r -> p (s r)"),
+                out=codes[:].rearrange("p s r -> p (s r)").bitcast(FP8X4),
+                scales=plane[:].rearrange("p s r -> p (s r)"),
                 in_=src.rearrange("p a r t -> p (a r t)"),
             )
+            for s in range(n):
+                operand[(g, quarters[s], negated)] = (codes[:, s, :], plane[:, s, :])
 
-        def negate(g):
-            nc.vector.tensor_scalar(
-                out=minus[g][:].rearrange("p a r t -> p (a r t)"),
-                in0=grouped[g][:, 1:4].rearrange("p a r t -> p (a r t)"),
-                scalar1=-1.0, scalar2=None, op0=mybir.AluOpType.mult,
-            )
+        def quantise_half(g, h):
+            quantise(g, grouped[(g, h)][:], (2 * h, 2 * h + 1), 0)
 
-        def quantise_minus(g):
-            quantise(g, minus[g][:, 0:2], 4, 2)
-            quantise(g, minus[g][:, 2:3], 6, 1)
+        def quantise_negated(g):
+            for h, first in ((0, 1), (1, 0)):
+                n = 2 - first
+                minus = keep.tile([P, n, P, 4], BF16, name="minus%d_%d" % (g, h), align_bytes=64)
+                nc.vector.tensor_scalar(
+                    out=minus[:].rearrange("p a r t -> p (a r t)"),
+                    in0=grouped[(g, h)][:, first:2].rearrange("p a r t -> p (a r t)"),
+                    scalar1=-1.0, scalar2=None, op0=mybir.AluOpType.mult,
+                )
+                quantise(g, minus[:], tuple(range(2 * h + first, 2 * h + 2)), 1)
 
-        done = {}
         acc = {}
+        done = {}
+        copies = [0]
 
-        def mx_pass(w, g, c, a):
-            b = a ^ w
-            n = done.get((c, b), 0)
-            done[(c, b)] = n + 1
-            slot = a + 3 if (w, a) in NEGATED else a
+        def open_block(c, b, lo, n, bank):
+            acc[(c, b, lo)] = psum.tile([P, n], F32, name="acc%d_%d_%d" % (c, b, lo), tag="bank%d" % bank)
+            done[(c, b, lo)] = 0
+
+        def mx_pass(w, g, c, a, lo=0, n=N_TILE):
+            key = (c, a ^ w, lo)
+            codes, plane = operand[(g, a, 1 if (w, a) in NEGATED else 0)]
+            t, first = w_sb[(w, g, c)]
             nc.tensor.matmul_mx(
-                out=acc[(c, b)][:],
-                lhsT=x_codes[g][:, slot, :].bitcast(FP8X4),
-                lhsT_scale=x_scales[g][:, slot, :],
-                rhs=w_sb[(w, g, c)][:].bitcast(FP8X4),
-                rhs_scale=planes[w][4 * g:P, N_TILE * c:N_TILE * (c + 1)],
-                start=(n == 0),
-                stop=(n == QUARTERS * GROUPS - 1),
+                out=acc[key][:],
+                lhsT=codes.bitcast(FP8X4),
+                lhsT_scale=plane,
+                rhs=t[:, first + 4 * lo:first + 4 * (lo + n)].bitcast(FP8X4),
+                rhs_scale=planes[w][4 * g:P, N_TILE * c + lo:N_TILE * c + lo + n],
+                start=(done[key] == 0),
+                stop=(done[key] == PASSES - 1),
             )
+            done[key] += 1
 
         def chunk(w, g, c):
-            order = [a for a in range(QUARTERS) if (w, a) not in NEGATED] + [a for a in range(QUARTERS) if (w, a) in NEGATED]
-            for a in order:
+            for a in range(QUARTERS):
                 mx_pass(w, g, c, a)
 
-        def leave(c, b):
-            dst = out_sb[c][:, N_TILE * b:N_TILE * (b + 1)]
-            if b % 2 == 0:
-                nc.vector.tensor_copy(out=dst, in_=acc[(c, b)][:])
+        def finish(c, b, lo=0, n=N_TILE):
+            res = keep.tile([P, n], F32, name="res%d_%d_%d" % (c, b, lo))
+            if copies[0] % 2 == 0:
+                nc.vector.tensor_copy(out=res[:], in_=acc[(c, b, lo)][:])
             else:
-                nc.scalar.copy(out=dst, in_=acc[(c, b)][:])
+                nc.scalar.copy(out=res[:], in_=acc[(c, b, lo)][:])
+            copies[0] += 1
+            nc.sync.dma_start(out=outs[c][:, N_TILE * b + lo:N_TILE * b + lo + n], in_=res[:])
 
-        def open_gate(c):
-            for b in range(4):
-                acc[(c, b)] = psum.tile([P, N_TILE], F32, name="acc%d_%d" % (c, b), tag="bank%d" % (4 * (c % 2) + b))
-
-        open_gate(0)
-        xt00 = transposes(0, 0, 4)
-        xt01 = transposes(0, 1, 5)
-        regroup(0, 0, xt00)
-        regroup(0, 1, xt01)
-        quantise(0, grouped[0][:, 0:2], 0, 2)
-        quantise(0, grouped[0][:, 2:4], 2, 2)
-        negate(0)
-        quantise_minus(0)
+        for b in range(4):
+            open_block(0, b, 0, N_TILE, b)
+        transposes(0, 0, 4)
+        transposes(0, 1, 5)
+        regroup(0, 0)
+        regroup(0, 1)
+        quantise_half(0, 0)
+        quantise_half(0, 1)
         chunk(0, 0, 0)
-        xt10 = transposes(1, 0, 6)
-        xt11 = transposes(1, 1, 7)
-        xt20 = transposes(2, 0, 4)
-        xt21 = transposes(2, 1, 5)
-        regroup(1, 0, xt10)
-        regroup(1, 1, xt11)
-        quantise(1, grouped[1][:, 0:2], 0, 2)
-        quantise(1, grouped[1][:, 2:4], 2, 2)
-        regroup(2, 0, xt20)
-        regroup(2, 1, xt21)
-        quantise(2, grouped[2][:, 0:2], 0, 2)
-        quantise(2, grouped[2][:, 2:4], 2, 2)
-        negate(1)
-        quantise_minus(1)
-        negate(2)
-        quantise_minus(2)
-        for w in range(4):
-            for g in range(GROUPS):
-                if (w, g) != (0, 0):
-                    chunk(w, g, 0)
+        quantise_negated(0)
+        transposes(1, 0, 6)
+        transposes(1, 1, 7)
+        transposes(2, 0, 4)
+        transposes(2, 1, 5)
+        for g in (1, 2):
+            regroup(g, 0)
+            regroup(g, 1)
+            quantise_half(g, 0)
+            quantise_half(g, 1)
+        quantise_negated(1)
+        quantise_negated(2)
+        chunk(0, 1, 0)
+        chunk(0, 2, 0)
         for b in range(4):
-            leave(0, b)
-        nc.sync.dma_start(out=outs[0][:, :], in_=out_sb[0][:])
+            open_block(1, b, 0, N_TILE, 4 + b)
+        for g in range(GROUPS):
+            chunk(0, g, 1)
+        for w in (1, 2):
+            for g in range(GROUPS):
+                for c in range(2):
+                    chunk(w, g, c)
+        for c in range(2):
+            for b in range(4):
+                for g in range(GROUPS):
+                    mx_pass(3, g, c, b ^ 3)
+                finish(c, b)
 
-        open_gate(1)
-        for w in range(4):
-            for g in range(GROUPS):
-                chunk(w, g, 1)
-        for b in range(4):
-            leave(1, b)
-        nc.sync.dma_start(out=outs[1][:, :], in_=out_sb[1][:])
-
-        open_gate(2)
-        for b in range(4):
-            for g in range(GROUPS):
-                for w in range(4):
-                    mx_pass(w, g, 2, b ^ w)
-            leave(2, b)
-            nc.sync.dma_start(
-                out=outs[2][:, N_TILE * b:N_TILE * (b + 1)],
-                in_=out_sb[2][:, N_TILE * b:N_TILE * (b + 1)],
-            )
+        pieces = [(0, 0, N_TILE, 0), (1, 0, N_TILE, 1), (2, 0, N_TILE, 2), (3, 0, 256, 3), (3, 256, 256, 4)]
+        for b, lo, n, bank in pieces:
+            open_block(2, b, lo, n, bank)
+            for w in range(4):
+                for g in range(GROUPS):
+                    mx_pass(w, g, 2, b ^ w, lo, n)
+            finish(2, b, lo, n)

@@ -16,6 +16,7 @@ GROUPS = 3
 N_TILE = 512
 PASSES = QUARTERS * GROUPS
 NEGATED = ((1, 3), (2, 1), (3, 2))
+WARM_FIRST = 6
 
 FLOPS = 2 * 128 * 6144 * 6144
 
@@ -36,29 +37,40 @@ def tile_quaternionlinearautograd_w_kernel(
         psum = ctx.enter_context(tc.psum_pool(name="psum", bufs=1))
         ctx.enter_context(tc.manual_schedule())
 
+        warm = keep.tile([P, N_TILE], BF16, name="warm")
+        nc.vector.memset(warm[:], 0.0)
         ident = keep.tile([P, P], F32, name="ident")
-        planes = [keep.tile([P, 3 * N_TILE], U8, name="planes%d" % w, align_bytes=64) for w in range(4)]
-        for w in range(4):
-            nc.vector.memset(planes[w][:].bitcast(I32), 0)
         make_identity(nc, ident[:])
+        plane_r = keep.tile([P, GROUPS, 3 * N_TILE], U8, name="plane_r", align_bytes=64)
+        nc.vector.memset(plane_r[:].rearrange("p g n -> p (g n)").bitcast(I32), 0)
+        packed = {}
+        for w in range(1, 4):
+            packed[w] = keep.tile([P, 3 * N_TILE], U8, name="packed%d" % w, align_bytes=64)
+            nc.vector.memset(packed[w][:].bitcast(I32), 0)
 
-        x_view = x.rearrange("b (a g k) -> g a b k", a=QUARTERS, g=GROUPS)
+        def weight_scales(w, g, first, n):
+            if w == 0:
+                return plane_r[:, g, first:first + n]
+            return packed[w][4 * g:P, first:first + n]
+
         x_sb = {}
 
-        def load_x(g, h):
-            x_sb[(g, h)] = keep.tile([P, 2, 512], BF16, name="x_sb%d_%d" % (g, h))
-            nc.sync.dma_start(
-                out=x_sb[(g, h)][:],
-                in_=x_view[g, 2 * h:2 * h + 2].rearrange("a b k -> b a k"),
-            )
+        def load_x(a):
+            x_sb[a] = keep.tile([P, GROUPS * 512], BF16, name="x_sb%d" % a)
+            nc.sync.dma_start(out=x_sb[a][:], in_=x[:, GROUPS * 512 * a:GROUPS * 512 * (a + 1)])
 
         def load_scales(w):
             for q in range(4):
-                dst = planes[w][32 * q:32 * q + 4 * GROUPS, :]
                 if w == 0:
-                    nc.sync.dma_start(out=dst.bitcast(I32), in_=scales[w].bitcast(I32)[:, 4 * q:4 * q + 4, :])
+                    nc.sync.dma_start(
+                        out=plane_r[32 * q:32 * q + 4].bitcast(I32),
+                        in_=scales[w].bitcast(I32)[:, 4 * q:4 * q + 4, :].rearrange("g r n -> r g n"),
+                    )
                 else:
-                    nc.gpsimd.dma_start(out=dst.bitcast(F32), in_=scales[w].bitcast(F32)[:, 4 * q:4 * q + 4, :])
+                    nc.gpsimd.dma_start(
+                        out=packed[w][32 * q:32 * q + 4 * GROUPS, :].bitcast(F32),
+                        in_=scales[w].bitcast(F32)[:, 4 * q:4 * q + 4, :],
+                    )
 
         w_sb = {}
 
@@ -72,19 +84,13 @@ def tile_quaternionlinearautograd_w_kernel(
             for c in range(c_count):
                 w_sb[(w, g, c_first + c)] = (t, 4 * N_TILE * c)
 
-        load_x(0, 0)
-        load_x(0, 1)
-        load_scales(0)
-        load_words(0, 0, 0, 1)
-        load_x(1, 0)
-        load_x(1, 1)
-        load_x(2, 0)
-        load_x(2, 1)
-        for w in range(1, 4):
+        for a in range(QUARTERS):
+            load_x(a)
+        for w in range(4):
             load_scales(w)
-        load_words(0, 1, 0, 2)
-        load_words(0, 2, 0, 2)
-        load_words(0, 0, 1, 1)
+        for c in range(2):
+            for g in range(GROUPS):
+                load_words(0, g, c, 1)
         for w in range(1, 4):
             for g in range(GROUPS):
                 load_words(w, g, 0, 2)
@@ -92,52 +98,63 @@ def tile_quaternionlinearautograd_w_kernel(
             for g in range(GROUPS):
                 load_words(w, g, 2, 1)
 
-        xt = {}
-        grouped = {}
         operand = {}
+        grouped = {}
 
-        def transposes(g, h, bank):
-            xt[(g, h)] = psum.tile([P, 4, P], F32, name="xt%d_%d" % (g, h), tag="bank%d" % bank)
-            xw = x_sb[(g, h)][:].bitcast(F32)
-            for al in range(2):
+        def dummy(n):
+            for d in range(n):
+                idle = psum.tile([P, N_TILE], F32, name="idle", tag="bank7")
+                nc.tensor.matmul(out=idle[:], lhsT=warm[:, 0:P], rhs=warm[:], start=True, stop=True)
+
+        def transposes(a, g_first, g_count, bank):
+            xt = psum.tile([P, 2 * g_count, P], F32, name="xt%d_%d" % (a, g_first), tag="bank%d" % bank)
+            xw = x_sb[a][:].bitcast(F32)
+            for s in range(g_count):
                 for u in range(2):
-                    nc.tensor.transpose(xt[(g, h)][:, 2 * al + u, :], xw[:, al, u:256:2], ident[:])
+                    g = g_first + s
+                    nc.tensor.transpose(xt[:, 2 * s + u, :], xw[:, 256 * g + u:256 * (g + 1):2], ident[:])
+            return xt
 
-        def regroup(g, h):
-            grouped[(g, h)] = keep.tile([P, 2, P, 4], BF16, name="grouped%d_%d" % (g, h), align_bytes=64)
-            dst = grouped[(g, h)][:].bitcast(F32)
-            src = xt[(g, h)][:].rearrange("p (a u) r -> p a r u", u=2)
-            if h == 0:
-                nc.vector.tensor_copy(out=dst, in_=src)
+        def regroup(a, g_first, g_count, xt, engine):
+            t = keep.tile([P, g_count, P, 4], BF16, name="grouped%d_%d" % (a, g_first), align_bytes=64)
+            grouped[(a, g_first)] = t
+            src = xt[:].rearrange("p (g u) r -> p g r u", u=2)
+            if engine == 0:
+                nc.vector.tensor_copy(out=t[:].bitcast(F32), in_=src)
             else:
-                nc.scalar.copy(out=dst, in_=src)
+                nc.scalar.copy(out=t[:].bitcast(F32), in_=src)
 
-        def quantise(g, src, quarters, negated):
-            n = len(quarters)
-            label = "%d_%d_%d" % (g, quarters[0], negated)
-            codes = keep.tile([P, n, P], U32, name="codes" + label, align_bytes=64)
-            plane = keep.tile([P, n, P], U8, name="plane" + label, align_bytes=64)
+        def quantise(a, g_first, g_count, src, negated):
+            label = "%d_%d_%d" % (a, g_first, negated)
+            codes = keep.tile([P, g_count, P], U32, name="codes" + label, align_bytes=64)
+            plane = keep.tile([P, g_count, P], U8, name="plane" + label, align_bytes=64)
             nc.vector.quantize_mx(
                 out=codes[:].rearrange("p s r -> p (s r)").bitcast(FP8X4),
                 scales=plane[:].rearrange("p s r -> p (s r)"),
-                in_=src.rearrange("p a r t -> p (a r t)"),
+                in_=src[:].rearrange("p g r t -> p (g r t)"),
             )
-            for s in range(n):
-                operand[(g, quarters[s], negated)] = (codes[:, s, :], plane[:, s, :])
+            for s in range(g_count):
+                operand[(g_first + s, a, negated)] = (codes[:, s, :], plane[:, s, :])
 
-        def quantise_half(g, h):
-            quantise(g, grouped[(g, h)][:], (2 * h, 2 * h + 1), 0)
+        def quantise_negated(a, g_first, g_count):
+            minus = keep.tile([P, g_count, P, 4], BF16, name="minus%d_%d" % (a, g_first), align_bytes=64)
+            nc.vector.tensor_scalar(
+                out=minus[:].rearrange("p g r t -> p (g r t)"),
+                in0=grouped[(a, g_first)][:].rearrange("p g r t -> p (g r t)"),
+                scalar1=-1.0, scalar2=None, op0=mybir.AluOpType.mult,
+            )
+            quantise(a, g_first, g_count, minus, 1)
 
-        def quantise_negated(g):
-            for h, first in ((0, 1), (1, 0)):
-                n = 2 - first
-                minus = keep.tile([P, n, P, 4], BF16, name="minus%d_%d" % (g, h), align_bytes=64)
-                nc.vector.tensor_scalar(
-                    out=minus[:].rearrange("p a r t -> p (a r t)"),
-                    in0=grouped[(g, h)][:, first:2].rearrange("p a r t -> p (a r t)"),
-                    scalar1=-1.0, scalar2=None, op0=mybir.AluOpType.mult,
-                )
-                quantise(g, minus[:], tuple(range(2 * h + first, 2 * h + 2)), 1)
+        dummy(WARM_FIRST)
+        for a in range(QUARTERS):
+            xt_two = transposes(a, 0, 2, 2 * a)
+            xt_one = transposes(a, 2, 1, 2 * a + 1)
+            if a < QUARTERS - 1:
+                dummy(1)
+            regroup(a, 0, 2, xt_two, 1)
+            regroup(a, 2, 1, xt_one, 0)
+            quantise(a, 0, 2, grouped[(a, 0)], 0)
+            quantise(a, 2, 1, grouped[(a, 2)], 0)
 
         acc = {}
         done = {}
@@ -156,7 +173,7 @@ def tile_quaternionlinearautograd_w_kernel(
                 lhsT=codes.bitcast(FP8X4),
                 lhsT_scale=plane,
                 rhs=t[:, first + 4 * lo:first + 4 * (lo + n)].bitcast(FP8X4),
-                rhs_scale=planes[w][4 * g:P, N_TILE * c + lo:N_TILE * c + lo + n],
+                rhs_scale=weight_scales(w, g, N_TILE * c + lo, n),
                 start=(done[key] == 0),
                 stop=(done[key] == PASSES - 1),
             )
@@ -175,33 +192,15 @@ def tile_quaternionlinearautograd_w_kernel(
             copies[0] += 1
             nc.sync.dma_start(out=outs[c][:, N_TILE * b + lo:N_TILE * b + lo + n], in_=res[:])
 
-        for b in range(4):
-            open_block(0, b, 0, N_TILE, b)
-        transposes(0, 0, 4)
-        transposes(0, 1, 5)
-        regroup(0, 0)
-        regroup(0, 1)
-        quantise_half(0, 0)
-        quantise_half(0, 1)
-        chunk(0, 0, 0)
-        quantise_negated(0)
-        transposes(1, 0, 6)
-        transposes(1, 1, 7)
-        transposes(2, 0, 4)
-        transposes(2, 1, 5)
-        for g in (1, 2):
-            regroup(g, 0)
-            regroup(g, 1)
-            quantise_half(g, 0)
-            quantise_half(g, 1)
-        quantise_negated(1)
-        quantise_negated(2)
-        chunk(0, 1, 0)
-        chunk(0, 2, 0)
-        for b in range(4):
-            open_block(1, b, 0, N_TILE, 4 + b)
-        for g in range(GROUPS):
-            chunk(0, g, 1)
+        for c in range(2):
+            for b in range(4):
+                open_block(c, b, 0, N_TILE, 4 * c + b)
+            for g in range(GROUPS):
+                chunk(0, g, c)
+            if c == 0:
+                for a in range(1, QUARTERS):
+                    quantise_negated(a, 0, 2)
+                    quantise_negated(a, 2, 1)
         for w in (1, 2):
             for g in range(GROUPS):
                 for c in range(2):

@@ -41,16 +41,21 @@ def tile_quaternionlinearautograd_w_kernel(
         nc.vector.memset(warm[:], 0.0)
         ident = keep.tile([P, P], F32, name="ident")
         make_identity(nc, ident[:])
-        plane_r = keep.tile([P, GROUPS, 3 * N_TILE], U8, name="plane_r", align_bytes=64)
-        nc.vector.memset(plane_r[:].rearrange("p g n -> p (g n)").bitcast(I32), 0)
+        plane_r = {}
+        for c_first, c_count in ((0, 1), (1, 2)):
+            t = keep.tile([P, GROUPS, N_TILE * c_count], U8, name="plane_r%d" % c_first, align_bytes=64)
+            nc.vector.memset(t[:].rearrange("p g n -> p (g n)").bitcast(I32), 0)
+            plane_r[c_first] = t
         packed = {}
         for w in range(1, 4):
             packed[w] = keep.tile([P, 3 * N_TILE], U8, name="packed%d" % w, align_bytes=64)
             nc.vector.memset(packed[w][:].bitcast(I32), 0)
 
         def weight_scales(w, g, first, n):
+            if w == 0 and first < N_TILE:
+                return plane_r[0][:, g, first:first + n]
             if w == 0:
-                return plane_r[:, g, first:first + n]
+                return plane_r[1][:, g, first - N_TILE:first - N_TILE + n]
             return packed[w][4 * g:P, first:first + n]
 
         x_sb = {}
@@ -62,9 +67,14 @@ def tile_quaternionlinearautograd_w_kernel(
         def load_scales(w):
             for q in range(4):
                 if w == 0:
+                    src = scales[w][:, 4 * q:4 * q + 4, :].rearrange("g r n -> r g n")
                     nc.sync.dma_start(
-                        out=plane_r[32 * q:32 * q + 4].bitcast(I32),
-                        in_=scales[w].bitcast(I32)[:, 4 * q:4 * q + 4, :].rearrange("g r n -> r g n"),
+                        out=plane_r[0][32 * q:32 * q + 4].bitcast(I32),
+                        in_=src[:, :, 0:N_TILE].bitcast(I32),
+                    )
+                    nc.gpsimd.dma_start(
+                        out=plane_r[1][32 * q:32 * q + 4].bitcast(F32),
+                        in_=src[:, :, N_TILE:3 * N_TILE].bitcast(F32),
                     )
                 else:
                     nc.gpsimd.dma_start(
@@ -195,26 +205,34 @@ def tile_quaternionlinearautograd_w_kernel(
         for c in range(2):
             for b in range(4):
                 open_block(c, b, 0, N_TILE, 4 * c + b)
-            for g in range(GROUPS):
-                chunk(0, g, c)
+            if c == 0:
+                for some in ((0, 1, 2), (3,)):
+                    for g in range(GROUPS):
+                        for a in some:
+                            mx_pass(0, g, c, a)
+            else:
+                for g in range(GROUPS):
+                    chunk(0, g, c)
             if c == 0:
                 for a in range(1, QUARTERS):
                     quantise_negated(a, 0, 2)
                     quantise_negated(a, 2, 1)
-        for w in (1, 2):
+        for w in (1, 2, 3):
             for g in range(GROUPS):
                 for c in range(2):
                     chunk(w, g, c)
         for c in range(2):
-            for b in range(4):
-                for g in range(GROUPS):
-                    mx_pass(3, g, c, b ^ 3)
-                finish(c, b)
+            for a in range(QUARTERS):
+                finish(c, a ^ 3)
 
-        pieces = [(0, 0, N_TILE, 0), (1, 0, N_TILE, 1), (2, 0, N_TILE, 2), (3, 0, 256, 3), (3, 256, 256, 4)]
+        pieces = [(0, 0, N_TILE, 0), (1, 0, N_TILE, 1), (2, 0, N_TILE, 2), (3, 0, 256, 3), (3, 256, 256, 7)]
         for b, lo, n, bank in pieces:
             open_block(2, b, lo, n, bank)
-            for w in range(4):
-                for g in range(GROUPS):
+        for w in range(3):
+            for g in range(GROUPS):
+                for b, lo, n, bank in pieces:
                     mx_pass(w, g, 2, b ^ w, lo, n)
+        for b, lo, n, bank in pieces:
+            for g in range(GROUPS):
+                mx_pass(3, g, 2, b ^ 3, lo, n)
             finish(2, b, lo, n)

@@ -16,7 +16,7 @@ GROUPS = 3
 N_TILE = 512
 PASSES = QUARTERS * GROUPS
 NEGATED = ((1, 3), (2, 1), (3, 2))
-WARM_FIRST = 6
+WARM_FIRST = 4
 
 FLOPS = 2 * 128 * 6144 * 6144
 
@@ -206,7 +206,7 @@ def tile_quaternionlinearautograd_w_kernel(
             for b in range(4):
                 open_block(c, b, 0, N_TILE, 4 * c + b)
             if c == 0:
-                for some in ((0, 1, 2), (3,)):
+                for some in ((0, 1), (2,), (3,)):
                     for g in range(GROUPS):
                         for a in some:
                             mx_pass(0, g, c, a)

@@ -17,6 +17,7 @@ N_TILE = 512
 PASSES = QUARTERS * GROUPS
 NEGATED = ((1, 3), (2, 1), (3, 2))
 WARM_FIRST = 4
+SCALE_SETS = ((0, 0, 1), (0, 1, 1), (1, 0, 2), (2, 0, 2), (3, 0, 2), (0, 2, 1), (1, 2, 1), (2, 2, 1), (3, 2, 1))
 
 FLOPS = 2 * 128 * 6144 * 6144
 
@@ -41,22 +42,16 @@ def tile_quaternionlinearautograd_w_kernel(
         nc.vector.memset(warm[:], 0.0)
         ident = keep.tile([P, P], F32, name="ident")
         make_identity(nc, ident[:])
-        plane_r = {}
-        for c_first, c_count in ((0, 1), (1, 2)):
-            t = keep.tile([P, GROUPS, N_TILE * c_count], U8, name="plane_r%d" % c_first, align_bytes=64)
+        w_plane = {}
+        for w, c_first, c_count in SCALE_SETS:
+            t = keep.tile([P, GROUPS, N_TILE * c_count], U8, name="plane%d_%d" % (w, c_first), align_bytes=64)
             nc.vector.memset(t[:].rearrange("p g n -> p (g n)").bitcast(I32), 0)
-            plane_r[c_first] = t
-        packed = {}
-        for w in range(1, 4):
-            packed[w] = keep.tile([P, 3 * N_TILE], U8, name="packed%d" % w, align_bytes=64)
-            nc.vector.memset(packed[w][:].bitcast(I32), 0)
+            for c in range(c_first, c_first + c_count):
+                w_plane[(w, c)] = (t, c_first)
 
         def weight_scales(w, g, first, n):
-            if w == 0 and first < N_TILE:
-                return plane_r[0][:, g, first:first + n]
-            if w == 0:
-                return plane_r[1][:, g, first - N_TILE:first - N_TILE + n]
-            return packed[w][4 * g:P, first:first + n]
+            t, c_first = w_plane[(w, first // N_TILE)]
+            return t[:, g, first - N_TILE * c_first:first - N_TILE * c_first + n]
 
         x_sb = {}
 
@@ -64,23 +59,14 @@ def tile_quaternionlinearautograd_w_kernel(
             x_sb[a] = keep.tile([P, GROUPS * 512], BF16, name="x_sb%d" % a)
             nc.sync.dma_start(out=x_sb[a][:], in_=x[:, GROUPS * 512 * a:GROUPS * 512 * (a + 1)])
 
-        def load_scales(w):
+        def load_scales(w, c_first, c_count):
+            t = w_plane[(w, c_first)][0]
             for q in range(4):
-                if w == 0:
-                    src = scales[w][:, 4 * q:4 * q + 4, :].rearrange("g r n -> r g n")
-                    nc.sync.dma_start(
-                        out=plane_r[0][32 * q:32 * q + 4].bitcast(I32),
-                        in_=src[:, :, 0:N_TILE].bitcast(I32),
-                    )
-                    nc.gpsimd.dma_start(
-                        out=plane_r[1][32 * q:32 * q + 4].bitcast(F32),
-                        in_=src[:, :, N_TILE:3 * N_TILE].bitcast(F32),
-                    )
-                else:
-                    nc.gpsimd.dma_start(
-                        out=packed[w][32 * q:32 * q + 4 * GROUPS, :].bitcast(F32),
-                        in_=scales[w].bitcast(F32)[:, 4 * q:4 * q + 4, :],
-                    )
+                src = scales[w][:, 4 * q:4 * q + 4, :].rearrange("g r n -> r g n")
+                nc.sync.dma_start(
+                    out=t[32 * q:32 * q + 4].bitcast(I32),
+                    in_=src[:, :, N_TILE * c_first:N_TILE * (c_first + c_count)].bitcast(I32),
+                )
 
         w_sb = {}
 
@@ -96,14 +82,16 @@ def tile_quaternionlinearautograd_w_kernel(
 
         for a in range(QUARTERS):
             load_x(a)
-        for w in range(4):
-            load_scales(w)
         for c in range(2):
+            load_scales(0, c, 1)
             for g in range(GROUPS):
                 load_words(0, g, c, 1)
         for w in range(1, 4):
+            load_scales(w, 0, 2)
             for g in range(GROUPS):
                 load_words(w, g, 0, 2)
+        for w in range(4):
+            load_scales(w, 2, 1)
         for w in range(4):
             for g in range(GROUPS):
                 load_words(w, g, 2, 1)

@@ -147,7 +147,7 @@ def tile_quaternionlinearautograd_w_kernel(
         for a in range(QUARTERS):
             xt_two = transposes(a, 0, 2, 2 * a)
             xt_one = transposes(a, 2, 1, 2 * a + 1)
-            if a < QUARTERS - 1:
+            if a == 1:
                 dummy(1)
             regroup(a, 0, 2, xt_two, 1)
             regroup(a, 2, 1, xt_one, 0)

@@ -92,7 +92,6 @@ def tile_quaternionlinearautograd_w_kernel(
                 load_words(w, g, 0, 2)
         for w in range(4):
             load_scales(w, 2, 1)
-        for w in range(4):
             for g in range(GROUPS):
                 load_words(w, g, 2, 1)
 
@@ -205,22 +204,20 @@ def tile_quaternionlinearautograd_w_kernel(
                 for a in range(1, QUARTERS):
                     quantise_negated(a, 0, 2)
                     quantise_negated(a, 2, 1)
-        for w in (1, 2, 3):
+        for w in (1, 2):
             for g in range(GROUPS):
                 for c in range(2):
                     chunk(w, g, c)
         for c in range(2):
+            for g in range(GROUPS):
+                chunk(3, g, c)
             for a in range(QUARTERS):
                 finish(c, a ^ 3)
 
-        pieces = [(0, 0, N_TILE, 0), (1, 0, N_TILE, 1), (2, 0, N_TILE, 2), (3, 0, 256, 3), (3, 256, 256, 7)]
+        pieces = [(0, 0, N_TILE, 0), (1, 0, N_TILE, 1), (2, 0, N_TILE, 2), (3, 0, 256, 3), (3, 256, 256, 0)]
         for b, lo, n, bank in pieces:
             open_block(2, b, lo, n, bank)
-        for w in range(3):
-            for g in range(GROUPS):
-                for b, lo, n, bank in pieces:
+            for w in range(4):
+                for g in range(GROUPS):
                     mx_pass(w, g, 2, b ^ w, lo, n)
-        for b, lo, n, bank in pieces:
-            for g in range(GROUPS):
-                mx_pass(3, g, 2, b ^ 3, lo, n)
             finish(2, b, lo, n)

@@ -214,10 +214,15 @@ def tile_quaternionlinearautograd_w_kernel(
             for a in range(QUARTERS):
                 finish(c, a ^ 3)
 
-        pieces = [(0, 0, N_TILE, 0), (1, 0, N_TILE, 1), (2, 0, N_TILE, 2), (3, 0, 256, 3), (3, 256, 256, 0)]
+        pieces = [(0, 0, N_TILE, 0), (1, 0, N_TILE, 1), (2, 0, N_TILE, 2), (3, 0, 256, 3), (3, 256, 256, 7)]
         for b, lo, n, bank in pieces:
             open_block(2, b, lo, n, bank)
-            for w in range(4):
+        for w in range(2):
+            for g in range(GROUPS):
+                for b, lo, n, bank in pieces:
+                    mx_pass(w, g, 2, b ^ w, lo, n)
+        for b, lo, n, bank in pieces:
+            for w in range(2, 4):
                 for g in range(GROUPS):
                     mx_pass(w, g, 2, b ^ w, lo, n)
             finish(2, b, lo, n)

from contextlib import ExitStack

import concourse.mybir as mybir
from concourse.masks import make_identity

F32 = mybir.dt.float32
BF16 = mybir.dt.bfloat16
I32 = mybir.dt.int32
U32 = mybir.dt.uint32
U8 = mybir.dt.uint8
FP8X4 = mybir.dt.float8_e4m3fn_x4

P = 128
QUARTERS = 4
GROUPS = 3
N_TILE = 512
PASSES = QUARTERS * GROUPS
NEGATED = ((1, 3), (2, 1), (3, 2))
WARM_FIRST = 4
SCALE_SETS = ((0, 0, 1), (0, 1, 1), (1, 0, 2), (2, 0, 2), (3, 0, 2), (0, 2, 1), (1, 2, 1), (2, 2, 1), (3, 2, 1))

FLOPS = 2 * 128 * 6144 * 6144


def tile_quaternionlinearautograd_w_kernel(
    tc, x,
    r_weight_words, r_weight_scales, i_weight_words, i_weight_scales,
    j_weight_words, j_weight_scales, k_weight_words, k_weight_scales,
    drop, out_0, out_1, out_2,
):
    nc = tc.nc
    words = (r_weight_words, i_weight_words, j_weight_words, k_weight_words)
    scales = (r_weight_scales, i_weight_scales, j_weight_scales, k_weight_scales)
    outs = (out_0, out_1, out_2)

    with ExitStack() as ctx:
        keep = ctx.enter_context(tc.tile_pool(name="keep", bufs=1))
        psum = ctx.enter_context(tc.psum_pool(name="psum", bufs=1))
        ctx.enter_context(tc.manual_schedule())

        warm = keep.tile([P, N_TILE], BF16, name="warm")
        nc.vector.memset(warm[:], 0.0)
        ident = keep.tile([P, P], F32, name="ident")
        make_identity(nc, ident[:])
        w_plane = {}
        for w, c_first, c_count in SCALE_SETS:
            t = keep.tile([P, GROUPS, N_TILE * c_count], U8, name="plane%d_%d" % (w, c_first), align_bytes=64)
            nc.vector.memset(t[:].rearrange("p g n -> p (g n)").bitcast(I32), 0)
            for c in range(c_first, c_first + c_count):
                w_plane[(w, c)] = (t, c_first)

        def weight_scales(w, g, first, n):
            t, c_first = w_plane[(w, first // N_TILE)]
            return t[:, g, first - N_TILE * c_first:first - N_TILE * c_first + n]

        x_sb = {}

        def load_x(a):
            x_sb[a] = keep.tile([P, GROUPS * 512], BF16, name="x_sb%d" % a)
            nc.sync.dma_start(out=x_sb[a][:], in_=x[:, GROUPS * 512 * a:GROUPS * 512 * (a + 1)])

        def load_scales(w, c_first, c_count):
            t = w_plane[(w, c_first)][0]
            for q in range(4):
                src = scales[w][:, 4 * q:4 * q + 4, :].rearrange("g r n -> r g n")
                nc.sync.dma_start(
                    out=t[32 * q:32 * q + 4].bitcast(I32),
                    in_=src[:, :, N_TILE * c_first:N_TILE * (c_first + c_count)].bitcast(I32),
                )

        w_sb = {}

        def load_words(w, g, c_first, c_count):
            t = keep.tile([P, 4 * N_TILE * c_count], U8, name="w_sb%d_%d_%d" % (w, g, c_first), align_bytes=64)
            src = words[w][g].rearrange("p n t -> p (n t)")
            nc.sync.dma_start(
                out=t[:].bitcast(I32),
                in_=src[:, 4 * N_TILE * c_first:4 * N_TILE * (c_first + c_count)].bitcast(I32),
            )
            for c in range(c_count):
                w_sb[(w, g, c_first + c)] = (t, 4 * N_TILE * c)

        for a in range(QUARTERS):
            load_x(a)
        for c in range(2):
            load_scales(0, c, 1)
            for g in range(GROUPS):
                load_words(0, g, c, 1)
        for w in range(1, 4):
            load_scales(w, 0, 2)
            for g in range(GROUPS):
                load_words(w, g, 0, 2)
        for w in range(4):
            load_scales(w, 2, 1)
            for g in range(GROUPS):
                load_words(w, g, 2, 1)

        operand = {}
        grouped = {}

        def dummy(n):
            for d in range(n):
                idle = psum.tile([P, N_TILE], F32, name="idle", tag="bank7")
                nc.tensor.matmul(out=idle[:], lhsT=warm[:, 0:P], rhs=warm[:], start=True, stop=True)

        def transposes(a, g_first, g_count, bank):
            xt = psum.tile([P, 2 * g_count, P], F32, name="xt%d_%d" % (a, g_first), tag="bank%d" % bank)
            xw = x_sb[a][:].bitcast(F32)
            for s in range(g_count):
                for u in range(2):
                    g = g_first + s
                    nc.tensor.transpose(xt[:, 2 * s + u, :], xw[:, 256 * g + u:256 * (g + 1):2], ident[:])
            return xt

        def regroup(a, g_first, g_count, xt, engine):
            t = keep.tile([P, g_count, P, 4], BF16, name="grouped%d_%d" % (a, g_first), align_bytes=64)
            grouped[(a, g_first)] = t
            src = xt[:].rearrange("p (g u) r -> p g r u", u=2)
            if engine == 0:
                nc.vector.tensor_copy(out=t[:].bitcast(F32), in_=src)
            else:
                nc.scalar.copy(out=t[:].bitcast(F32), in_=src)

        def quantise(a, g_first, g_count, src, negated):
            label = "%d_%d_%d" % (a, g_first, negated)
            codes = keep.tile([P, g_count, P], U32, name="codes" + label, align_bytes=64)
            plane = keep.tile([P, g_count, P], U8, name="plane" + label, align_bytes=64)
            nc.vector.quantize_mx(
                out=codes[:].rearrange("p s r -> p (s r)").bitcast(FP8X4),
                scales=plane[:].rearrange("p s r -> p (s r)"),
                in_=src[:].rearrange("p g r t -> p (g r t)"),
            )
            for s in range(g_count):
                operand[(g_first + s, a, negated)] = (codes[:, s, :], plane[:, s, :])

        def quantise_negated(a, g_first, g_count):
            minus = keep.tile([P, g_count, P, 4], BF16, name="minus%d_%d" % (a, g_first), align_bytes=64)
            nc.vector.tensor_scalar(
                out=minus[:].rearrange("p g r t -> p (g r t)"),
                in0=grouped[(a, g_first)][:].rearrange("p g r t -> p (g r t)"),
                scalar1=-1.0, scalar2=None, op0=mybir.AluOpType.mult,
            )
            quantise(a, g_first, g_count, minus, 1)

        dummy(WARM_FIRST)
        for a in range(QUARTERS):
            xt_two = transposes(a, 0, 2, 2 * a)
            xt_one = transposes(a, 2, 1, 2 * a + 1)
            if a == 1:
                dummy(1)
            regroup(a, 0, 2, xt_two, 1)
            regroup(a, 2, 1, xt_one, 0)
            quantise(a, 0, 2, grouped[(a, 0)], 0)
            quantise(a, 2, 1, grouped[(a, 2)], 0)

        acc = {}
        done = {}
        copies = [0]

        def open_block(c, b, lo, n, bank):
            acc[(c, b, lo)] = psum.tile([P, n], F32, name="acc%d_%d_%d" % (c, b, lo), tag="bank%d" % bank)
            done[(c, b, lo)] = 0

        def mx_pass(w, g, c, a, lo=0, n=N_TILE):
            key = (c, a ^ w, lo)
            codes, plane = operand[(g, a, 1 if (w, a) in NEGATED else 0)]
            t, first = w_sb[(w, g, c)]
            nc.tensor.matmul_mx(
                out=acc[key][:],
                lhsT=codes.bitcast(FP8X4),
                lhsT_scale=plane,
                rhs=t[:, first + 4 * lo:first + 4 * (lo + n)].bitcast(FP8X4),
                rhs_scale=weight_scales(w, g, N_TILE * c + lo, n),
                start=(done[key] == 0),
                stop=(done[key] == PASSES - 1),
            )
            done[key] += 1

        def chunk(w, g, c):
            for a in range(QUARTERS):
                mx_pass(w, g, c, a)

        def finish(c, b, lo=0, n=N_TILE):
            res = keep.tile([P, n], F32, name="res%d_%d_%d" % (c, b, lo))
            if copies[0] % 2 == 0:
                nc.vector.tensor_copy(out=res[:], in_=acc[(c, b, lo)][:])
            else:
                nc.scalar.copy(out=res[:], in_=acc[(c, b, lo)][:])
            copies[0] += 1
            nc.sync.dma_start(out=outs[c][:, N_TILE * b + lo:N_TILE * b + lo + n], in_=res[:])

        for c in range(2):
            for b in range(4):
                open_block(c, b, 0, N_TILE, 4 * c + b)
            if c == 0:
                for some in ((0, 1), (2,), (3,)):
                    for g in range(GROUPS):
                        for a in some:
                            mx_pass(0, g, c, a)
            else:
                for g in range(GROUPS):
                    chunk(0, g, c)
            if c == 0:
                for a in range(1, QUARTERS):
                    quantise_negated(a, 0, 2)
                    quantise_negated(a, 2, 1)
        for w in (1, 2):
            for g in range(GROUPS):
                for c in range(2):
                    chunk(w, g, c)
        for c in range(2):
            for g in range(GROUPS):
                chunk(3, g, c)
            for a in range(QUARTERS):
                finish(c, a ^ 3)

        pieces = [(0, 0, N_TILE, 0), (1, 0, N_TILE, 1), (2, 0, N_TILE, 2), (3, 0, 256, 3), (3, 256, 256, 7)]
        for b, lo, n, bank in pieces:
            open_block(2, b, lo, n, bank)
        for w in range(2):
            for g in range(GROUPS):
                for b, lo, n, bank in pieces:
                    mx_pass(w, g, 2, b ^ w, lo, n)
        for b, lo, n, bank in pieces:
            for w in range(2, 4):
                for g in range(GROUPS):
                    mx_pass(w, g, 2, b ^ w, lo, n)
            finish(2, b, lo, n)
